import numpy as np
import ml_dtypes


def mxq(x, axis, fmt="e4m3"):
    dtype, down = {"e4m3": (ml_dtypes.float8_e4m3fn, 7), "e5m2": (ml_dtypes.float8_e5m2, 14)}[fmt]
    v = np.moveaxis(np.asarray(x, np.float32).astype(ml_dtypes.bfloat16).astype(np.float64), axis, -1)
    blocks = v.reshape(v.shape[:-1] + (-1, 32))
    amax = np.abs(blocks).max(-1, keepdims=True)
    byte = np.maximum(np.where(amax > 0, np.frexp(amax)[1] - 1 + 127, 0) - down, 1)
    scale = np.exp2(byte - 127.0)
    codes = (blocks / scale).astype(np.float32).astype(dtype).astype(np.float64)
    return np.moveaxis((codes * scale).reshape(v.shape), -1, axis)


WIDE = False


def mx_kscale(k):
    if not WIDE:
        return np.ones(k)
    levels = np.array([10, -10, 5, -5, 0])
    if k % 512:
        return np.exp2(np.random.permutation(np.resize(levels, k // 32))).repeat(32)
    a = np.empty((k // 512, 16))
    for p in range(k // 512):
        a[p, :8] = np.random.permutation(np.resize(levels, 8))
        for g in range(8):
            far = levels[np.abs(levels - a[p, g]) >= 10]
            a[p, g + 8] = far[np.random.randint(len(far))]
    return np.exp2(a.ravel()).repeat(32)


BF16 = ml_dtypes.bfloat16


def bf(x):
    return np.asarray(x, np.float32).astype(BF16)


def f64(x):
    return np.asarray(x).astype(np.float64)


B, S, D, H, DH, F = 4, 2048, 1024, 2, 64, 4096
E = H * DH
EPS = 1e-5


def layernorm(x, g, b):
    mu = x.mean(-1, keepdims=True)
    var = np.square(x - mu).mean(-1, keepdims=True)
    return (x - mu) / np.sqrt(var + EPS) * g + b


def make_pe():
    position = np.arange(S)[:, None] * 1.0
    div_term = np.exp(np.arange(0, DH, 2) * -(np.log(10000.0) / DH))
    pe = np.zeros((S, DH))
    pe[:, 0::2] = np.sin(position * div_term)
    pe[:, 1::2] = np.cos(position * div_term)
    return pe


def rope(t, pe):
    tr = t.reshape(B, H, S, DH // 2, 2)
    c = pe[:S, 0::2][None, None]
    d = pe[:S, 1::2][None, None]
    t0 = tr[..., 0] * c - tr[..., 1] * d
    t1 = tr[..., 0] * d + tr[..., 1] * c
    return np.stack([t0, t1], axis=-1).reshape(B, H, S, DH)


def setup_inputs():
    s = mx_kscale(D)
    x = np.random.standard_normal((B, S, D)) + 0.5 * np.random.standard_normal((B, S, 1))
    return {"x": bf(x),
            "pe": bf(make_pe()),
            "w_qkv": bf(np.random.standard_normal((3 * E, D)) / np.sqrt(D) / s),
            "g1": bf((1.0 + 0.1 * np.random.standard_normal(D)) * s),
            "b1": bf(0.1 * np.random.standard_normal(D) * s)}


def reference(x, pe, w_qkv, g1, b1):
    h = layernorm(f64(x), f64(g1), f64(b1))
    qkv = mxq(h, 2, "e4m3") @ mxq(f64(w_qkv), 1, "e4m3").T
    qkv = qkv.reshape(B, S, 3, H, DH)
    q, k, v = [qkv[:, :, i].transpose(0, 2, 1, 3) for i in range(3)]
    p = f64(pe)
    return rope(q, p), rope(k, p), v

@@ -1,0 +1,378 @@
+from contextlib import ExitStack
+
+import concourse.mybir as mybir
+from concourse.masks import make_identity
+
+F32 = mybir.dt.float32
+BF16 = mybir.dt.bfloat16
+U32 = mybir.dt.uint32
+U8 = mybir.dt.uint8
+FP8X4 = mybir.dt.float8_e4m3fn_x4
+ALU = mybir.AluOpType
+ACT = mybir.ActivationFunctionType
+
+B, S, D, H, DH = 4, 2048, 1024, 2, 64
+EPS = 1e-5
+P = 128
+PACK = 4
+PASSES = D // (P * PACK)
+CHUNKS = D // P
+SLOTS_PER_BATCH = S // P
+SLOTS = 4
+TOKENS = SLOTS * P
+GROUPS_PER_BATCH = SLOTS_PER_BATCH // SLOTS
+PAIRS = DH // 2
+ROTATED = 2 * H
+QK_COLS = ROTATED * DH
+V_COLS = H * DH
+OUT_COLS = QK_COLS + V_COLS
+BN_MAX = 512
+BN_VALUES = 6
+LOADS_AHEAD = 2
+
+FLOPS = 2 * B * S * D * OUT_COLS
+
+
+def tile_minitransformerlayer_pa_t_kernel(tc, x, pe, w_qkv, g1, b1, out_0, out_1, out_2):
+    nc = tc.nc
+    outs = (out_0, out_1, out_2)
+
+    with ExitStack() as ctx:
+        const = ctx.enter_context(tc.tile_pool(name="const", bufs=1))
+        x_pool = ctx.enter_context(tc.tile_pool(name="x_pool", bufs=4))
+        small = ctx.enter_context(tc.tile_pool(name="small", bufs=3))
+        xn_pool = ctx.enter_context(tc.tile_pool(name="xn_pool", bufs=2))
+        h_pool = ctx.enter_context(tc.tile_pool(name="h_pool", bufs=2))
+        mx_pool = ctx.enter_context(tc.tile_pool(name="mx_pool", bufs=2))
+        rot_pool = ctx.enter_context(tc.tile_pool(name="rot_pool", bufs=4))
+        res_pool = ctx.enter_context(tc.tile_pool(name="res_pool", bufs=3))
+
+        groups = []
+        for index in range(B * GROUPS_PER_BATCH):
+            batch, first_slot = index // GROUPS_PER_BATCH, (index % GROUPS_PER_BATCH) * SLOTS
+            if index in (0, B * GROUPS_PER_BATCH - 1):
+                groups.append((batch, first_slot, SLOTS // 2))
+                groups.append((batch, first_slot + SLOTS // 2, SLOTS // 2))
+            else:
+                groups.append((batch, first_slot, SLOTS))
+
+        live = {}
+
+        def load_group(group):
+            batch, first_slot, count = groups[group]
+            x_sb = x_pool.tile([P, SLOTS, D], BF16, name="x_sb")
+            by_slot = x[batch].rearrange("(p t) k -> p t k", t=SLOTS_PER_BATCH)
+            for s in range(count):
+                nc.sync.dma_start(out=x_sb[:, s, :], in_=by_slot[:, first_slot + s, :])
+            live["x", group] = x_sb
+
+        xt_psum = ctx.enter_context(tc.psum_pool(name="xt_psum", bufs=4))
+        qk_psum = ctx.enter_context(tc.psum_pool(name="qk_psum", bufs=2))
+        v_psum = ctx.enter_context(tc.psum_pool(name="v_psum", bufs=2))
+
+        ident_f32 = const.tile([P, P], F32, name="ident_f32")
+        eps = const.tile([P, 1], F32, name="eps")
+        gain_bf16 = const.tile([P, PASSES, PACK], BF16, name="gain_bf16")
+        bias_bf16 = const.tile([P, PASSES, PACK], BF16, name="bias_bf16")
+        w_sb = const.tile([P, OUT_COLS // P, D], BF16, name="w_sb")
+        pe_sb = const.tile([P, SLOTS_PER_BATCH, PAIRS, 2], BF16, name="pe_sb")
+        c_twice = const.tile([P, SLOTS_PER_BATCH, PAIRS, 2], F32, name="c_twice")
+        d_pos = const.tile([P, SLOTS_PER_BATCH, PAIRS], F32, name="d_pos")
+        d_neg = const.tile([P, SLOTS_PER_BATCH, PAIRS], F32, name="d_neg")
+        gain_bias = const.tile([P, 2 * CHUNKS], F32, name="gain_bias")
+        w_grouped = const.tile([P, PASSES, OUT_COLS, PACK], BF16, name="w_grouped", align_bytes=64)
+        w_codes = const.tile([P, PASSES, OUT_COLS], U32, name="w_codes", align_bytes=64)
+        w_scales = const.tile([P, PASSES, OUT_COLS], U8, name="w_scales", align_bytes=64)
+
+        def load_constants():
+            nc.vector.memset(eps[:], EPS)
+            for landed, vec in ((gain_bf16, g1), (bias_bf16, b1)):
+                nc.sync.dma_start(out=landed[:], in_=vec.rearrange("(u p t) -> p u t", p=P, t=PACK))
+            nc.sync.dma_start(out=w_sb[:], in_=w_qkv.rearrange("(i p) k -> p i k", p=P))
+            nc.sync.dma_start(
+                out=pe_sb[:], in_=pe.rearrange("(p t) (j e) -> p t j e", t=SLOTS_PER_BATCH, e=2)
+            )
+
+        def rotation_tables():
+            make_identity(nc, ident_f32[:])
+            nc.gpsimd.tensor_scalar(
+                out=c_twice[:],
+                in0=pe_sb[:, :, :, 0:1].to_broadcast([P, SLOTS_PER_BATCH, PAIRS, 2]),
+                scalar1=1.0,
+                scalar2=0.0,
+                op0=ALU.mult,
+                op1=ALU.add,
+            )
+            for table, sign in ((d_pos, 1.0), (d_neg, -1.0)):
+                nc.gpsimd.tensor_scalar(
+                    out=table[:], in0=pe_sb[:, :, :, 1], scalar1=sign, scalar2=0.0, op0=ALU.mult, op1=ALU.add
+                )
+
+        def transpose_constants():
+            for first, landed in ((0, gain_bf16), (CHUNKS, bias_bf16)):
+                nc.vector.tensor_copy(
+                    out=gain_bias[:, first : first + CHUNKS], in_=landed[:].rearrange("p u t -> p (u t)")
+                )
+            w_words = w_sb[:].bitcast(F32)
+            pass_words = D // 2 // PASSES
+            for u in range(PASSES):
+                for i in range(OUT_COLS // P):
+                    w_t = xt_psum.tile([P, 2, P], F32, name="w_t", tag="xn_t")
+                    for e in range(2):
+                        nc.tensor.transpose(
+                            w_t[:, e, :],
+                            w_words[:, i, u * pass_words + e : (u + 1) * pass_words : 2],
+                            ident_f32[:],
+                        )
+                    nc.scalar.copy(
+                        out=w_grouped[:, u, i * P : (i + 1) * P, :].rearrange("p n t -> p (n t)").bitcast(F32),
+                        in_=w_t[:].rearrange("p e n -> p n e"),
+                    )
+
+        def quantise_weights():
+            for u in range(PASSES):
+                for i in range(OUT_COLS // P):
+                    rows = slice(i * P, (i + 1) * P)
+                    nc.vector.quantize_mx(
+                        out=w_codes[:, u, rows].bitcast(FP8X4),
+                        scales=w_scales[:, u, rows],
+                        in_=w_grouped[:, u, rows, :].rearrange("p n t -> p (n t)"),
+                    )
+
+        def statistics(group):
+            count = groups[group][2]
+            x_sb = live["x", group]
+            stats = small.tile([P, SLOTS, D // BN_MAX, BN_VALUES], F32, name="stats")
+            mean_var = small.tile([P, SLOTS, 2], F32, name="mean_var")
+            for s in range(count):
+                for part in range(D // BN_MAX):
+                    nc.vector.bn_stats(
+                        out=stats[:, s, part, :], in_=x_sb[:, s, part * BN_MAX : (part + 1) * BN_MAX]
+                    )
+            for s in range(count):
+                nc.vector.bn_aggr(out=mean_var[:, s, :], in_=stats[:, s].rearrange("p a c -> p (a c)"))
+            live["mean_var", group] = mean_var
+
+        def standard_deviation(group):
+            count = groups[group][2]
+            std = small.tile([P, SLOTS], F32, name="std")
+            nc.scalar.activation(
+                out=std[:, 0:count],
+                in_=live["mean_var", group][:, 0:count, 1],
+                func=ACT.Sqrt,
+                bias=eps[:],
+                scale=1.0,
+            )
+            live["std", group] = std
+
+        def reciprocal_std(group):
+            count = groups[group][2]
+            rstd = small.tile([P, SLOTS], F32, name="rstd")
+            nc.vector.reciprocal(out=rstd[:, 0:count], in_=live["std", group][:, 0:count])
+            live["rstd", group] = rstd
+
+        def negated_mean(group):
+            count = groups[group][2]
+            neg_mean = small.tile([P, SLOTS], F32, name="neg_mean")
+            nc.gpsimd.tensor_scalar(
+                out=neg_mean[:, 0:count],
+                in0=live["mean_var", group][:, 0:count, 0],
+                scalar1=-1.0,
+                scalar2=0.0,
+                op0=ALU.mult,
+                op1=ALU.add,
+            )
+            live["neg_mean", group] = neg_mean
+
+        def normalise(group):
+            xn = xn_pool.tile([P, SLOTS, D], F32, name="xn")
+            for s in range(groups[group][2]):
+                nc.gpsimd.tensor_scalar(
+                    out=xn[:, s, :].rearrange("p (u t k) -> p u t k", u=PASSES, t=PACK),
+                    in0=live["x", group][:, s, :].rearrange("p (u k t) -> p u t k", u=PASSES, t=PACK),
+                    scalar1=live["neg_mean", group][:, s : s + 1],
+                    scalar2=live["rstd", group][:, s : s + 1],
+                    op0=ALU.add,
+                    op1=ALU.mult,
+                )
+            live["xn", group] = xn
+
+        def transpose_and_scale(group, chunks):
+            count = groups[group][2]
+            if chunks[0] == 0:
+                live["h_chunks", group] = h_pool.tile([P, CHUNKS, TOKENS], BF16, name="h_chunks")
+            xn, h_chunks = live["xn", group], live["h_chunks", group]
+            for c in chunks:
+                xn_t = xt_psum.tile([P, TOKENS], F32, name="xn_t")
+                for s in range(count):
+                    nc.tensor.transpose(
+                        xn_t[:, s * P : (s + 1) * P], xn[:, s, c * P : (c + 1) * P], ident_f32[:]
+                    )
+                nc.scalar.activation(
+                    out=h_chunks[:, c, 0 : count * P],
+                    in_=xn_t[:, 0 : count * P],
+                    func=ACT.Identity,
+                    scale=gain_bias[:, c : c + 1],
+                    bias=gain_bias[:, CHUNKS + c : CHUNKS + c + 1],
+                )
+
+        def regroup(group, u):
+            tokens = groups[group][2] * P
+            if u == 0:
+                live["h_grouped", group] = h_pool.tile(
+                    [P, PASSES, TOKENS, PACK], BF16, name="h_grouped", align_bytes=64
+                )
+            nc.scalar.copy(
+                out=live["h_grouped", group][:, u, 0:tokens, :].rearrange("p (n i) t -> p n t i", i=4),
+                in_=live["h_chunks", group][:, u * PACK : (u + 1) * PACK, 0:tokens].rearrange(
+                    "p t (n i) -> p n t i", i=4
+                ),
+            )
+
+        def quantise(group):
+            tokens = groups[group][2] * P
+            h_codes = mx_pool.tile([P, PASSES, TOKENS], U32, name="h_codes", align_bytes=64)
+            h_scales = mx_pool.tile([P, PASSES, TOKENS], U8, name="h_scales", align_bytes=64)
+            for u in range(PASSES):
+                nc.vector.quantize_mx(
+                    out=h_codes[:, u, 0:tokens].bitcast(FP8X4),
+                    scales=h_scales[:, u, 0:tokens],
+                    in_=live["h_grouped", group][:, u, 0:tokens, :].rearrange("p n t -> p (n t)"),
+                )
+            live["h_codes", group] = h_codes
+            live["h_scales", group] = h_scales
+
+        def project(group):
+            h_codes, h_scales = live["h_codes", group], live["h_scales", group]
+            v_ps = v_psum.tile([P, SLOTS, V_COLS], F32, name="v_ps")
+            live["v_ps", group] = v_ps
+            for half in range(groups[group][2] // 2):
+                qk_ps = qk_psum.tile([P, 2, QK_COLS], F32, name="qk_ps")
+                live["qk_ps", group, half] = qk_ps
+                for i in range(2):
+                    s = 2 * half + i
+                    tokens = slice(s * P, (s + 1) * P)
+                    for acc, cols in (
+                        (qk_ps[:, i, :], slice(0, QK_COLS)),
+                        (v_ps[:, s, :], slice(QK_COLS, OUT_COLS)),
+                    ):
+                        for u in range(PASSES):
+                            nc.tensor.matmul_mx(
+                                out=acc,
+                                lhsT=h_codes[:, u, tokens].bitcast(FP8X4),
+                                lhsT_scale=h_scales[:, u, tokens],
+                                rhs=w_codes[:, u, cols].bitcast(FP8X4),
+                                rhs_scale=w_scales[:, u, cols],
+                                start=(u == 0),
+                                stop=(u == PASSES - 1),
+                            )
+
+        def rotation_products(group, half):
+            if half == 0:
+                live["result", group] = res_pool.tile([P, 3 * H, SLOTS, DH], F32, name="result")
+            first_slot = groups[group][1] + 2 * half
+            slots = slice(first_slot, first_slot + 2)
+            qk_ps = live["qk_ps", group, half]
+            rotated = live["result", group][:, 0:ROTATED, 2 * half : 2 * half + 2, :]
+            nc.vector.tensor_tensor(
+                out=rotated.rearrange("p a i d -> p i a d"),
+                in0=qk_ps[:].rearrange("p i (a d) -> p i a d", a=ROTATED),
+                in1=c_twice[:, slots]
+                .rearrange("p i j e -> p i (j e)")
+                .unsqueeze(2)
+                .to_broadcast([P, 2, ROTATED, DH]),
+                op=ALU.mult,
+            )
+            by_pair = qk_ps[:].rearrange("p i (a j e) -> p i a j e", a=ROTATED, e=2)
+            crossed = rot_pool.tile([P, 2, 2, ROTATED, PAIRS], F32, name="crossed")
+            nc.vector.tensor_tensor(
+                out=crossed[:, 0],
+                in0=by_pair[:, :, :, :, 1],
+                in1=d_neg[:, slots].unsqueeze(2).to_broadcast([P, 2, ROTATED, PAIRS]),
+                op=ALU.mult,
+            )
+            nc.vector.tensor_tensor(
+                out=crossed[:, 1],
+                in0=by_pair[:, :, :, :, 0],
+                in1=d_pos[:, slots].unsqueeze(2).to_broadcast([P, 2, ROTATED, PAIRS]),
+                op=ALU.mult,
+            )
+            live["crossed", group, half] = crossed
+
+        def rotation_sum(group, half, engine):
+            rotated = live["result", group][:, 0:ROTATED, 2 * half : 2 * half + 2, :]
+            engine.tensor_tensor(
+                out=rotated.rearrange("p a i (j e) -> p i a j e", e=2),
+                in0=rotated.rearrange("p a i (j e) -> p i a j e", e=2),
+                in1=live["crossed", group, half][:].rearrange("p e i a j -> p i a j e"),
+                op=ALU.add,
+            )
+
+        def copy_v(group):
+            count = groups[group][2]
+            nc.vector.tensor_copy(
+                out=live["result", group][:, ROTATED : 3 * H, 0:count, :].rearrange("p a s d -> p s a d"),
+                in_=live["v_ps", group][:, 0:count, :].rearrange("p s (a d) -> p s a d", a=H),
+            )
+
+        def store(group):
+            batch, first_slot, count = groups[group]
+            for which in range(3):
+                by_slot = outs[which][batch].rearrange("h (p t) d -> p h t d", t=SLOTS_PER_BATCH)
+                nc.sync.dma_start(
+                    out=by_slot[:, :, first_slot : first_slot + count, :],
+                    in_=live["result", group][:, which * H : (which + 1) * H, 0:count, :],
+                )
+
+        def in_range(group):
+            return 0 <= group < len(groups)
+
+        def is_whole(group):
+            return in_range(group) and groups[group][2] == SLOTS
+
+        with tc.manual_schedule():
+            load_group(0)
+            load_constants()
+            for group in range(1, 1 + LOADS_AHEAD):
+                load_group(group)
+            rotation_tables()
+            statistics(0)
+            negated_mean(0)
+            standard_deviation(0)
+            reciprocal_std(0)
+            transpose_constants()
+            quantise_weights()
+
+            for r in range(len(groups) + 3):
+                if in_range(r + 1 + LOADS_AHEAD):
+                    load_group(r + 1 + LOADS_AHEAD)
+                if in_range(r):
+                    normalise(r)
+                if in_range(r + 1):
+                    statistics(r + 1)
+                    negated_mean(r + 1)
+                if in_range(r - 1):
+                    transpose_and_scale(r - 1, range(CHUNKS))
+                if in_range(r + 1):
+                    standard_deviation(r + 1)
+                if in_range(r - 2):
+                    quantise(r - 2)
+                if is_whole(r - 4):
+                    rotation_sum(r - 4, 1, nc.vector)
+                    store(r - 4)
+                if in_range(r - 1):
+                    regroup(r - 1, 0)
+                    regroup(r - 1, 1)
+                if in_range(r - 3):
+                    rotation_products(r - 3, 0)
+                    rotation_sum(r - 3, 0, nc.gpsimd)
+                if in_range(r + 1):
+                    reciprocal_std(r + 1)
+                if is_whole(r - 3):
+                    rotation_products(r - 3, 1)
+                if in_range(r - 3):
+                    copy_v(r - 3)
+                if in_range(r - 2):
+                    project(r - 2)
+                if in_range(r - 3) and not is_whole(r - 3):
+                    store(r - 3)

@@ -188,8 +188,8 @@ def tile_minitransformerlayer_pa_t_kernel(tc, x, pe, w_qkv, g1, b1, out_0, out_1
             xn = xn_pool.tile([P, SLOTS, D], F32, name="xn")
             for s in range(groups[group][2]):
                 nc.gpsimd.tensor_scalar(
-                    out=xn[:, s, :].rearrange("p (u t k) -> p u t k", u=PASSES, t=PACK),
-                    in0=live["x", group][:, s, :].rearrange("p (u k t) -> p u t k", u=PASSES, t=PACK),
+                    out=xn[:, s, :],
+                    in0=live["x", group][:, s, :],
                     scalar1=live["neg_mean", group][:, s : s + 1],
                     scalar2=live["rstd", group][:, s : s + 1],
                     op0=ALU.add,
@@ -204,9 +204,10 @@ def tile_minitransformerlayer_pa_t_kernel(tc, x, pe, w_qkv, g1, b1, out_0, out_1
             xn, h_chunks = live["xn", group], live["h_chunks", group]
             for c in chunks:
                 xn_t = xt_psum.tile([P, TOKENS], F32, name="xn_t")
+                by_chunk = xn[:].rearrange("p s (u k t) -> p s u t k", u=PASSES, t=PACK)
                 for s in range(count):
                     nc.tensor.transpose(
-                        xn_t[:, s * P : (s + 1) * P], xn[:, s, c * P : (c + 1) * P], ident_f32[:]
+                        xn_t[:, s * P : (s + 1) * P], by_chunk[:, s, c // PACK, c % PACK, :], ident_f32[:]
                     )
                 nc.scalar.activation(
                     out=h_chunks[:, c, 0 : count * P],

@@ -28,7 +28,11 @@ V_COLS = H * DH
 OUT_COLS = QK_COLS + V_COLS
 BN_MAX = 512
 BN_VALUES = 6
-LOADS_AHEAD = 2
+LOADS_AHEAD = 4
+FIRST_SIZES = [2, 2]
+LAST_SIZES = [2, 2]
+CHUNKS_AHEAD = 3
+VECTOR_CHUNKS = 1
 
 FLOPS = 2 * B * S * D * OUT_COLS
 
@@ -39,8 +43,8 @@ def tile_minitransformerlayer_pa_t_kernel(tc, x, pe, w_qkv, g1, b1, out_0, out_1
 
     with ExitStack() as ctx:
         const = ctx.enter_context(tc.tile_pool(name="const", bufs=1))
-        x_pool = ctx.enter_context(tc.tile_pool(name="x_pool", bufs=4))
-        small = ctx.enter_context(tc.tile_pool(name="small", bufs=3))
+        x_pool = ctx.enter_context(tc.tile_pool(name="x_pool", bufs=LOADS_AHEAD + 2))
+        small = ctx.enter_context(tc.tile_pool(name="small", bufs=4))
         xn_pool = ctx.enter_context(tc.tile_pool(name="xn_pool", bufs=2))
         h_pool = ctx.enter_context(tc.tile_pool(name="h_pool", bufs=2))
         mx_pool = ctx.enter_context(tc.tile_pool(name="mx_pool", bufs=2))
@@ -48,13 +52,22 @@ def tile_minitransformerlayer_pa_t_kernel(tc, x, pe, w_qkv, g1, b1, out_0, out_1
         res_pool = ctx.enter_context(tc.tile_pool(name="res_pool", bufs=3))
 
         groups = []
-        for index in range(B * GROUPS_PER_BATCH):
-            batch, first_slot = index // GROUPS_PER_BATCH, (index % GROUPS_PER_BATCH) * SLOTS
-            if index in (0, B * GROUPS_PER_BATCH - 1):
-                groups.append((batch, first_slot, SLOTS // 2))
-                groups.append((batch, first_slot + SLOTS // 2, SLOTS // 2))
-            else:
-                groups.append((batch, first_slot, SLOTS))
+        for batch in range(B):
+            sizes = [SLOTS] * GROUPS_PER_BATCH
+            if batch == 0:
+                sizes[0:1] = FIRST_SIZES
+            if batch == B - 1:
+                sizes[-1:] = LAST_SIZES
+            first_slot = 0
+            for count in sizes:
+                groups.append((batch, first_slot, count))
+                first_slot += count
+
+        def halves(group):
+            return range((groups[group][2] + 1) // 2)
+
+        def slots_of_half(group, half):
+            return min(2, groups[group][2] - 2 * half)
 
         live = {}
 
@@ -77,24 +90,25 @@ def tile_minitransformerlayer_pa_t_kernel(tc, x, pe, w_qkv, g1, b1, out_0, out_1
         w_sb = const.tile([P, OUT_COLS // P, D], BF16, name="w_sb")
         pe_sb = const.tile([P, SLOTS_PER_BATCH, PAIRS, 2], BF16, name="pe_sb")
         c_twice = const.tile([P, SLOTS_PER_BATCH, PAIRS, 2], F32, name="c_twice")
-        d_pos = const.tile([P, SLOTS_PER_BATCH, PAIRS], F32, name="d_pos")
-        d_neg = const.tile([P, SLOTS_PER_BATCH, PAIRS], F32, name="d_neg")
+        d_signed = const.tile([P, SLOTS_PER_BATCH, PAIRS, 2], F32, name="d_signed")
         gain_bias = const.tile([P, 2 * CHUNKS], F32, name="gain_bias")
         w_grouped = const.tile([P, PASSES, OUT_COLS, PACK], BF16, name="w_grouped", align_bytes=64)
         w_codes = const.tile([P, PASSES, OUT_COLS], U32, name="w_codes", align_bytes=64)
         w_scales = const.tile([P, PASSES, OUT_COLS], U8, name="w_scales", align_bytes=64)
 
-        def load_constants():
-            nc.vector.memset(eps[:], EPS)
+        def load_gains():
             for landed, vec in ((gain_bf16, g1), (bias_bf16, b1)):
                 nc.sync.dma_start(out=landed[:], in_=vec.rearrange("(u p t) -> p u t", p=P, t=PACK))
+
+        def load_weights():
             nc.sync.dma_start(out=w_sb[:], in_=w_qkv.rearrange("(i p) k -> p i k", p=P))
+
+        def load_tables():
             nc.sync.dma_start(
                 out=pe_sb[:], in_=pe.rearrange("(p t) (j e) -> p t j e", t=SLOTS_PER_BATCH, e=2)
             )
 
         def rotation_tables():
-            make_identity(nc, ident_f32[:])
             nc.gpsimd.tensor_scalar(
                 out=c_twice[:],
                 in0=pe_sb[:, :, :, 0:1].to_broadcast([P, SLOTS_PER_BATCH, PAIRS, 2]),
@@ -103,9 +117,14 @@ def tile_minitransformerlayer_pa_t_kernel(tc, x, pe, w_qkv, g1, b1, out_0, out_1
                 op0=ALU.mult,
                 op1=ALU.add,
             )
-            for table, sign in ((d_pos, 1.0), (d_neg, -1.0)):
+            for member, sign in ((0, -1.0), (1, 1.0)):
                 nc.gpsimd.tensor_scalar(
-                    out=table[:], in0=pe_sb[:, :, :, 1], scalar1=sign, scalar2=0.0, op0=ALU.mult, op1=ALU.add
+                    out=d_signed[:, :, :, member],
+                    in0=pe_sb[:, :, :, 1],
+                    scalar1=sign,
+                    scalar2=0.0,
+                    op0=ALU.mult,
+                    op1=ALU.add,
                 )
 
         def transpose_constants():
@@ -197,31 +216,39 @@ def tile_minitransformerlayer_pa_t_kernel(tc, x, pe, w_qkv, g1, b1, out_0, out_1
                 )
             live["xn", group] = xn
 
-        def transpose_and_scale(group, chunks):
-            count = groups[group][2]
-            if chunks[0] == 0:
-                live["h_chunks", group] = h_pool.tile([P, CHUNKS, TOKENS], BF16, name="h_chunks")
-            xn, h_chunks = live["xn", group], live["h_chunks", group]
+        def transpose_chunks(group, chunks):
+            by_chunk = live["xn", group][:].rearrange("p s (u k t) -> p s u t k", u=PASSES, t=PACK)
             for c in chunks:
                 xn_t = xt_psum.tile([P, TOKENS], F32, name="xn_t")
-                by_chunk = xn[:].rearrange("p s (u k t) -> p s u t k", u=PASSES, t=PACK)
-                for s in range(count):
+                for s in range(groups[group][2]):
                     nc.tensor.transpose(
                         xn_t[:, s * P : (s + 1) * P], by_chunk[:, s, c // PACK, c % PACK, :], ident_f32[:]
                     )
-                nc.scalar.activation(
-                    out=h_chunks[:, c, 0 : count * P],
-                    in_=xn_t[:, 0 : count * P],
-                    func=ACT.Identity,
-                    scale=gain_bias[:, c : c + 1],
-                    bias=gain_bias[:, CHUNKS + c : CHUNKS + c + 1],
-                )
+                live["xn_t", group, c] = xn_t
+
+        def scalar_chunks(group):
+            return CHUNKS - VECTOR_CHUNKS if groups[group][2] == SLOTS else CHUNKS
+
+        def scale_and_shift(group, chunks, engine):
+            tokens = groups[group][2] * P
+            if ("h_chunks", group) not in live:
+                live["h_chunks", group] = h_pool.tile([P, CHUNKS, TOKENS], BF16, name="h_chunks")
+            for c in chunks:
+                out = live["h_chunks", group][:, c, 0:tokens]
+                in_ = live["xn_t", group, c][:, 0:tokens]
+                gain, bias = gain_bias[:, c : c + 1], gain_bias[:, CHUNKS + c : CHUNKS + c + 1]
+                if engine is nc.scalar:
+                    nc.scalar.activation(out=out, in_=in_, func=ACT.Identity, scale=gain, bias=bias)
+                else:
+                    nc.vector.tensor_scalar(
+                        out=out, in0=in_, scalar1=gain, scalar2=bias, op0=ALU.mult, op1=ALU.add
+                    )
 
         def regroup(group, u):
             tokens = groups[group][2] * P
             if u == 0:
                 live["h_grouped", group] = h_pool.tile(
-                    [P, PASSES, TOKENS, PACK], BF16, name="h_grouped", align_bytes=64
+                    [P, PASSES, tokens, PACK], BF16, name="h_grouped", align_bytes=64
                 )
             nc.scalar.copy(
                 out=live["h_grouped", group][:, u, 0:tokens, :].rearrange("p (n i) t -> p n t i", i=4),
@@ -232,14 +259,13 @@ def tile_minitransformerlayer_pa_t_kernel(tc, x, pe, w_qkv, g1, b1, out_0, out_1
 
         def quantise(group):
             tokens = groups[group][2] * P
-            h_codes = mx_pool.tile([P, PASSES, TOKENS], U32, name="h_codes", align_bytes=64)
-            h_scales = mx_pool.tile([P, PASSES, TOKENS], U8, name="h_scales", align_bytes=64)
-            for u in range(PASSES):
-                nc.vector.quantize_mx(
-                    out=h_codes[:, u, 0:tokens].bitcast(FP8X4),
-                    scales=h_scales[:, u, 0:tokens],
-                    in_=live["h_grouped", group][:, u, 0:tokens, :].rearrange("p n t -> p (n t)"),
-                )
+            h_codes = mx_pool.tile([P, PASSES, tokens], U32, name="h_codes", align_bytes=64)
+            h_scales = mx_pool.tile([P, PASSES, tokens], U8, name="h_scales", align_bytes=64)
+            nc.vector.quantize_mx(
+                out=h_codes[:].rearrange("p u n -> p (u n)").bitcast(FP8X4),
+                scales=h_scales[:].rearrange("p u n -> p (u n)"),
+                in_=live["h_grouped", group][:].rearrange("p u n t -> p (u n t)"),
+            )
             live["h_codes", group] = h_codes
             live["h_scales", group] = h_scales
 
@@ -247,10 +273,10 @@ def tile_minitransformerlayer_pa_t_kernel(tc, x, pe, w_qkv, g1, b1, out_0, out_1
             h_codes, h_scales = live["h_codes", group], live["h_scales", group]
             v_ps = v_psum.tile([P, SLOTS, V_COLS], F32, name="v_ps")
             live["v_ps", group] = v_ps
-            for half in range(groups[group][2] // 2):
+            for half in halves(group):
                 qk_ps = qk_psum.tile([P, 2, QK_COLS], F32, name="qk_ps")
                 live["qk_ps", group, half] = qk_ps
-                for i in range(2):
+                for i in range(slots_of_half(group, half)):
                     s = 2 * half + i
                     tokens = slice(s * P, (s + 1) * P)
                     for acc, cols in (
@@ -271,41 +297,41 @@ def tile_minitransformerlayer_pa_t_kernel(tc, x, pe, w_qkv, g1, b1, out_0, out_1
         def rotation_products(group, half):
             if half == 0:
                 live["result", group] = res_pool.tile([P, 3 * H, SLOTS, DH], F32, name="result")
+            count = slots_of_half(group, half)
             first_slot = groups[group][1] + 2 * half
-            slots = slice(first_slot, first_slot + 2)
-            qk_ps = live["qk_ps", group, half]
-            rotated = live["result", group][:, 0:ROTATED, 2 * half : 2 * half + 2, :]
+            slots = slice(first_slot, first_slot + count)
+            qk_ps = live["qk_ps", group, half][:, 0:count]
+            rotated = live["result", group][:, 0:ROTATED, 2 * half : 2 * half + count, :]
             nc.vector.tensor_tensor(
                 out=rotated.rearrange("p a i d -> p i a d"),
-                in0=qk_ps[:].rearrange("p i (a d) -> p i a d", a=ROTATED),
+                in0=qk_ps.rearrange("p i (a d) -> p i a d", a=ROTATED),
                 in1=c_twice[:, slots]
                 .rearrange("p i j e -> p i (j e)")
                 .unsqueeze(2)
-                .to_broadcast([P, 2, ROTATED, DH]),
+                .to_broadcast([P, count, ROTATED, DH]),
                 op=ALU.mult,
             )
-            by_pair = qk_ps[:].rearrange("p i (a j e) -> p i a j e", a=ROTATED, e=2)
-            crossed = rot_pool.tile([P, 2, 2, ROTATED, PAIRS], F32, name="crossed")
+            by_pair = qk_ps.rearrange("p i (a j e) -> p i a j e", a=ROTATED, e=2)
+            crossed = rot_pool.tile([P, 2, ROTATED, PAIRS, 2], F32, name="crossed")
             nc.vector.tensor_tensor(
-                out=crossed[:, 0],
-                in0=by_pair[:, :, :, :, 1],
-                in1=d_neg[:, slots].unsqueeze(2).to_broadcast([P, 2, ROTATED, PAIRS]),
-                op=ALU.mult,
-            )
-            nc.vector.tensor_tensor(
-                out=crossed[:, 1],
-                in0=by_pair[:, :, :, :, 0],
-                in1=d_pos[:, slots].unsqueeze(2).to_broadcast([P, 2, ROTATED, PAIRS]),
+                out=crossed[:, 0:count],
+                in0=by_pair[:, :, :, :, ::-1],
+                in1=d_signed[:, slots]
+                .rearrange("p i j e -> p i (j e)")
+                .unsqueeze(2)
+                .to_broadcast([P, count, ROTATED, DH])
+                .rearrange("p i a (j e) -> p i a j e", e=2),
                 op=ALU.mult,
             )
             live["crossed", group, half] = crossed
 
         def rotation_sum(group, half, engine):
-            rotated = live["result", group][:, 0:ROTATED, 2 * half : 2 * half + 2, :]
+            count = slots_of_half(group, half)
+            rotated = live["result", group][:, 0:ROTATED, 2 * half : 2 * half + count, :]
             engine.tensor_tensor(
-                out=rotated.rearrange("p a i (j e) -> p i a j e", e=2),
-                in0=rotated.rearrange("p a i (j e) -> p i a j e", e=2),
-                in1=live["crossed", group, half][:].rearrange("p e i a j -> p i a j e"),
+                out=rotated.rearrange("p a i d -> p i a d"),
+                in0=rotated.rearrange("p a i d -> p i a d"),
+                in1=live["crossed", group, half][:, 0:count].rearrange("p i a j e -> p i a (j e)"),
                 op=ALU.add,
             )
 
@@ -328,52 +354,57 @@ def tile_minitransformerlayer_pa_t_kernel(tc, x, pe, w_qkv, g1, b1, out_0, out_1
         def in_range(group):
             return 0 <= group < len(groups)
 
-        def is_whole(group):
-            return in_range(group) and groups[group][2] == SLOTS
+        def is_last(group):
+            return group >= len(groups) - len(LAST_SIZES)
 
         with tc.manual_schedule():
+            nc.vector.memset(eps[:], EPS)
+            make_identity(nc, ident_f32[:])
             load_group(0)
-            load_constants()
-            for group in range(1, 1 + LOADS_AHEAD):
-                load_group(group)
-            rotation_tables()
-            statistics(0)
-            negated_mean(0)
-            standard_deviation(0)
-            reciprocal_std(0)
-            transpose_constants()
-            quantise_weights()
+            load_gains()
+            load_group(1)
+            load_weights()
+            load_group(2)
+            load_tables()
 
-            for r in range(len(groups) + 3):
-                if in_range(r + 1 + LOADS_AHEAD):
-                    load_group(r + 1 + LOADS_AHEAD)
+            for r in range(-1, len(groups) + 3):
+                if in_range(r + LOADS_AHEAD) and r + LOADS_AHEAD > 2:
+                    load_group(r + LOADS_AHEAD)
                 if in_range(r):
+                    reciprocal_std(r)
                     normalise(r)
+                if in_range(r - 4) and not is_last(r - 4):
+                    for half in halves(r - 4):
+                        rotation_sum(r - 4, half, nc.gpsimd)
+                    store(r - 4)
+                if r == 1:
+                    rotation_tables()
                 if in_range(r + 1):
                     statistics(r + 1)
                     negated_mean(r + 1)
                 if in_range(r - 1):
-                    transpose_and_scale(r - 1, range(CHUNKS))
+                    transpose_chunks(r - 1, range(CHUNKS_AHEAD, CHUNKS))
+                    scale_and_shift(r - 1, range(scalar_chunks(r - 1)), nc.scalar)
                 if in_range(r + 1):
                     standard_deviation(r + 1)
-                if in_range(r - 2):
-                    quantise(r - 2)
-                if is_whole(r - 4):
-                    rotation_sum(r - 4, 1, nc.vector)
-                    store(r - 4)
+                if r == -1:
+                    transpose_constants()
+                if in_range(r - 3):
+                    for half in halves(r - 3):
+                        rotation_products(r - 3, half)
+                    copy_v(r - 3)
+                    if is_last(r - 3):
+                        for half in halves(r - 3):
+                            rotation_sum(r - 3, half, nc.vector)
+                        store(r - 3)
                 if in_range(r - 1):
+                    scale_and_shift(r - 1, range(scalar_chunks(r - 1), CHUNKS), nc.vector)
                     regroup(r - 1, 0)
                     regroup(r - 1, 1)
-                if in_range(r - 3):
-                    rotation_products(r - 3, 0)
-                    rotation_sum(r - 3, 0, nc.gpsimd)
-                if in_range(r + 1):
-                    reciprocal_std(r + 1)
-                if is_whole(r - 3):
-                    rotation_products(r - 3, 1)
-                if in_range(r - 3):
-                    copy_v(r - 3)
+                if in_range(r):
+                    transpose_chunks(r, range(CHUNKS_AHEAD))
+                if r == 1:
+                    quantise_weights()
                 if in_range(r - 2):
+                    quantise(r - 2)
                     project(r - 2)
-                if in_range(r - 3) and not is_whole(r - 3):
-                    store(r - 3)

@@ -32,7 +32,7 @@ LOADS_AHEAD = 4
 FIRST_SIZES = [2, 2]
 LAST_SIZES = [2, 2]
 CHUNKS_AHEAD = 3
-VECTOR_CHUNKS = 1
+VECTOR_CHUNKS = 0
 
 FLOPS = 2 * B * S * D * OUT_COLS
 

@@ -28,11 +28,10 @@ V_COLS = H * DH
 OUT_COLS = QK_COLS + V_COLS
 BN_MAX = 512
 BN_VALUES = 6
-LOADS_AHEAD = 4
+LOADS_AHEAD = 5
 FIRST_SIZES = [2, 2]
 LAST_SIZES = [2, 2]
-CHUNKS_AHEAD = 3
-VECTOR_CHUNKS = 0
+CHUNKS_AHEAD = 4
 
 FLOPS = 2 * B * S * D * OUT_COLS
 
@@ -44,7 +43,7 @@ def tile_minitransformerlayer_pa_t_kernel(tc, x, pe, w_qkv, g1, b1, out_0, out_1
     with ExitStack() as ctx:
         const = ctx.enter_context(tc.tile_pool(name="const", bufs=1))
         x_pool = ctx.enter_context(tc.tile_pool(name="x_pool", bufs=LOADS_AHEAD + 2))
-        small = ctx.enter_context(tc.tile_pool(name="small", bufs=4))
+        small = ctx.enter_context(tc.tile_pool(name="small", bufs=5))
         xn_pool = ctx.enter_context(tc.tile_pool(name="xn_pool", bufs=2))
         h_pool = ctx.enter_context(tc.tile_pool(name="h_pool", bufs=2))
         mx_pool = ctx.enter_context(tc.tile_pool(name="mx_pool", bufs=2))
@@ -226,23 +225,18 @@ def tile_minitransformerlayer_pa_t_kernel(tc, x, pe, w_qkv, g1, b1, out_0, out_1
                     )
                 live["xn_t", group, c] = xn_t
 
-        def scalar_chunks(group):
-            return CHUNKS - VECTOR_CHUNKS if groups[group][2] == SLOTS else CHUNKS
-
-        def scale_and_shift(group, chunks, engine):
+        def scale_and_shift(group):
             tokens = groups[group][2] * P
-            if ("h_chunks", group) not in live:
-                live["h_chunks", group] = h_pool.tile([P, CHUNKS, TOKENS], BF16, name="h_chunks")
-            for c in chunks:
-                out = live["h_chunks", group][:, c, 0:tokens]
-                in_ = live["xn_t", group, c][:, 0:tokens]
-                gain, bias = gain_bias[:, c : c + 1], gain_bias[:, CHUNKS + c : CHUNKS + c + 1]
-                if engine is nc.scalar:
-                    nc.scalar.activation(out=out, in_=in_, func=ACT.Identity, scale=gain, bias=bias)
-                else:
-                    nc.vector.tensor_scalar(
-                        out=out, in0=in_, scalar1=gain, scalar2=bias, op0=ALU.mult, op1=ALU.add
-                    )
+            h_chunks = h_pool.tile([P, CHUNKS, TOKENS], BF16, name="h_chunks")
+            for c in range(CHUNKS):
+                nc.scalar.activation(
+                    out=h_chunks[:, c, 0:tokens],
+                    in_=live["xn_t", group, c][:, 0:tokens],
+                    func=ACT.Identity,
+                    scale=gain_bias[:, c : c + 1],
+                    bias=gain_bias[:, CHUNKS + c : CHUNKS + c + 1],
+                )
+            live["h_chunks", group] = h_chunks
 
         def regroup(group, u):
             tokens = groups[group][2] * P
@@ -367,44 +361,48 @@ def tile_minitransformerlayer_pa_t_kernel(tc, x, pe, w_qkv, g1, b1, out_0, out_1
             load_group(2)
             load_tables()
 
-            for r in range(-1, len(groups) + 3):
-                if in_range(r + LOADS_AHEAD) and r + LOADS_AHEAD > 2:
+            for r in range(-2, len(groups) + 3):
+                if in_range(r + LOADS_AHEAD):
                     load_group(r + LOADS_AHEAD)
-                if in_range(r):
-                    reciprocal_std(r)
-                    normalise(r)
                 if in_range(r - 4) and not is_last(r - 4):
-                    for half in halves(r - 4):
+                    for half in halves(r - 4)[1:]:
                         rotation_sum(r - 4, half, nc.gpsimd)
                     store(r - 4)
-                if r == 1:
-                    rotation_tables()
-                if in_range(r + 1):
-                    statistics(r + 1)
-                    negated_mean(r + 1)
+                if in_range(r):
+                    normalise(r)
                 if in_range(r - 1):
                     transpose_chunks(r - 1, range(CHUNKS_AHEAD, CHUNKS))
-                    scale_and_shift(r - 1, range(scalar_chunks(r - 1)), nc.scalar)
-                if in_range(r + 1):
-                    standard_deviation(r + 1)
-                if r == -1:
-                    transpose_constants()
+                    scale_and_shift(r - 1)
                 if in_range(r - 3):
                     for half in halves(r - 3):
                         rotation_products(r - 3, half)
-                    copy_v(r - 3)
-                    if is_last(r - 3):
-                        for half in halves(r - 3):
-                            rotation_sum(r - 3, half, nc.vector)
-                        store(r - 3)
+                if in_range(r + 1):
+                    negated_mean(r + 1)
+                    standard_deviation(r + 1)
                 if in_range(r - 1):
-                    scale_and_shift(r - 1, range(scalar_chunks(r - 1), CHUNKS), nc.vector)
                     regroup(r - 1, 0)
                     regroup(r - 1, 1)
                 if in_range(r):
                     transpose_chunks(r, range(CHUNKS_AHEAD))
-                if r == 1:
+                if r == 2:
                     quantise_weights()
                 if in_range(r - 2):
                     quantise(r - 2)
                     project(r - 2)
+                if in_range(r - 3):
+                    rotation_sum(r - 3, 0, nc.vector)
+                if in_range(r - 3) and is_last(r - 3):
+                    for half in halves(r - 3)[1:]:
+                        rotation_sum(r - 3, half, nc.vector)
+                    copy_v(r - 3)
+                    store(r - 3)
+                if in_range(r + 1):
+                    reciprocal_std(r + 1)
+                if in_range(r + 2):
+                    statistics(r + 2)
+                if r == -1:
+                    transpose_constants()
+                if r == 0:
+                    rotation_tables()
+                if in_range(r - 3) and not is_last(r - 3):
+                    copy_v(r - 3)

@@ -30,7 +30,7 @@ BN_MAX = 512
 BN_VALUES = 6
 LOADS_AHEAD = 5
 FIRST_SIZES = [2, 2]
-LAST_SIZES = [2, 2]
+LAST_SIZES = [2, 1, 1]
 CHUNKS_AHEAD = 4
 
 FLOPS = 2 * B * S * D * OUT_COLS
@@ -171,22 +171,16 @@ def tile_minitransformerlayer_pa_t_kernel(tc, x, pe, w_qkv, g1, b1, out_0, out_1
                 nc.vector.bn_aggr(out=mean_var[:, s, :], in_=stats[:, s].rearrange("p a c -> p (a c)"))
             live["mean_var", group] = mean_var
 
-        def standard_deviation(group):
-            count = groups[group][2]
-            std = small.tile([P, SLOTS], F32, name="std")
-            nc.scalar.activation(
-                out=std[:, 0:count],
-                in_=live["mean_var", group][:, 0:count, 1],
-                func=ACT.Sqrt,
-                bias=eps[:],
-                scale=1.0,
-            )
-            live["std", group] = std
-
         def reciprocal_std(group):
             count = groups[group][2]
             rstd = small.tile([P, SLOTS], F32, name="rstd")
-            nc.vector.reciprocal(out=rstd[:, 0:count], in_=live["std", group][:, 0:count])
+            nc.scalar.activation(
+                out=rstd[:, 0:count],
+                in_=live["mean_var", group][:, 0:count, 1],
+                func=ACT.Abs_reciprocal_sqrt,
+                bias=eps[:],
+                scale=1.0,
+            )
             live["rstd", group] = rstd
 
         def negated_mean(group):
@@ -378,7 +372,7 @@ def tile_minitransformerlayer_pa_t_kernel(tc, x, pe, w_qkv, g1, b1, out_0, out_1
                         rotation_products(r - 3, half)
                 if in_range(r + 1):
                     negated_mean(r + 1)
-                    standard_deviation(r + 1)
+                    reciprocal_std(r + 1)
                 if in_range(r - 1):
                     regroup(r - 1, 0)
                     regroup(r - 1, 1)
@@ -396,8 +390,6 @@ def tile_minitransformerlayer_pa_t_kernel(tc, x, pe, w_qkv, g1, b1, out_0, out_1
                         rotation_sum(r - 3, half, nc.vector)
                     copy_v(r - 3)
                     store(r - 3)
-                if in_range(r + 1):
-                    reciprocal_std(r + 1)
                 if in_range(r + 2):
                     statistics(r + 2)
                 if r == -1:

@@ -31,7 +31,10 @@ BN_VALUES = 6
 LOADS_AHEAD = 5
 FIRST_SIZES = [2, 2]
 LAST_SIZES = [2, 1, 1]
-CHUNKS_AHEAD = 4
+BANKS_FOR_TRANSPOSES = 4
+GROUPS_AT_END = 4
+VECTOR_CHUNKS_AT_END = 3
+ROUNDS_TO_FILL = 2
 
 FLOPS = 2 * B * S * D * OUT_COLS
 
@@ -78,7 +81,7 @@ def tile_minitransformerlayer_pa_t_kernel(tc, x, pe, w_qkv, g1, b1, out_0, out_1
                 nc.sync.dma_start(out=x_sb[:, s, :], in_=by_slot[:, first_slot + s, :])
             live["x", group] = x_sb
 
-        xt_psum = ctx.enter_context(tc.psum_pool(name="xt_psum", bufs=4))
+        xt_psum = ctx.enter_context(tc.psum_pool(name="xt_psum", bufs=BANKS_FOR_TRANSPOSES))
         qk_psum = ctx.enter_context(tc.psum_pool(name="qk_psum", bufs=2))
         v_psum = ctx.enter_context(tc.psum_pool(name="v_psum", bufs=2))
 
@@ -157,57 +160,75 @@ def tile_minitransformerlayer_pa_t_kernel(tc, x, pe, w_qkv, g1, b1, out_0, out_1
                         in_=w_grouped[:, u, rows, :].rearrange("p n t -> p (n t)"),
                     )
 
+        def slots_at_once(group):
+            count = groups[group][2]
+            step = 1 if group == 0 else 2 if group == len(FIRST_SIZES) else count
+            return [range(s, s + step) for s in range(0, count, step)]
+
         def statistics(group):
             count = groups[group][2]
             x_sb = live["x", group]
             stats = small.tile([P, SLOTS, D // BN_MAX, BN_VALUES], F32, name="stats")
             mean_var = small.tile([P, SLOTS, 2], F32, name="mean_var")
-            for s in range(count):
-                for part in range(D // BN_MAX):
-                    nc.vector.bn_stats(
-                        out=stats[:, s, part, :], in_=x_sb[:, s, part * BN_MAX : (part + 1) * BN_MAX]
-                    )
-            for s in range(count):
-                nc.vector.bn_aggr(out=mean_var[:, s, :], in_=stats[:, s].rearrange("p a c -> p (a c)"))
+            for slots in slots_at_once(group):
+                for s in slots:
+                    for part in range(D // BN_MAX):
+                        nc.vector.bn_stats(
+                            out=stats[:, s, part, :], in_=x_sb[:, s, part * BN_MAX : (part + 1) * BN_MAX]
+                        )
+                for s in slots:
+                    nc.vector.bn_aggr(out=mean_var[:, s, :], in_=stats[:, s].rearrange("p a c -> p (a c)"))
             live["mean_var", group] = mean_var
 
-        def reciprocal_std(group):
-            count = groups[group][2]
-            rstd = small.tile([P, SLOTS], F32, name="rstd")
+        def reciprocal_std(group, slots):
+            if ("rstd", group) not in live:
+                live["rstd", group] = small.tile([P, SLOTS], F32, name="rstd")
             nc.scalar.activation(
-                out=rstd[:, 0:count],
-                in_=live["mean_var", group][:, 0:count, 1],
+                out=live["rstd", group][:, slots.start : slots.stop],
+                in_=live["mean_var", group][:, slots.start : slots.stop, 1],
                 func=ACT.Abs_reciprocal_sqrt,
                 bias=eps[:],
                 scale=1.0,
             )
-            live["rstd", group] = rstd
 
-        def negated_mean(group):
-            count = groups[group][2]
-            neg_mean = small.tile([P, SLOTS], F32, name="neg_mean")
+        def negated_mean(group, slots):
+            if ("neg_mean", group) not in live:
+                live["neg_mean", group] = small.tile([P, SLOTS], F32, name="neg_mean")
             nc.gpsimd.tensor_scalar(
-                out=neg_mean[:, 0:count],
-                in0=live["mean_var", group][:, 0:count, 0],
+                out=live["neg_mean", group][:, slots.start : slots.stop],
+                in0=live["mean_var", group][:, slots.start : slots.stop, 0],
                 scalar1=-1.0,
                 scalar2=0.0,
                 op0=ALU.mult,
                 op1=ALU.add,
             )
-            live["neg_mean", group] = neg_mean
 
-        def normalise(group):
-            xn = xn_pool.tile([P, SLOTS, D], F32, name="xn")
-            for s in range(groups[group][2]):
+        def normalise_on_vector(group, slot):
+            live["xn", group] = xn_pool.tile([P, SLOTS, D], F32, name="xn")
+            nc.vector.tensor_scalar(
+                out=live["xn", group][:, slot, :],
+                in0=live["x", group][:, slot, :],
+                scalar1=live["mean_var", group][:, slot, 0:1],
+                scalar2=live["rstd", group][:, slot : slot + 1],
+                op0=ALU.subtract,
+                op1=ALU.mult,
+            )
+
+        def normalise(group, slots):
+            if ("xn", group) not in live:
+                live["xn", group] = xn_pool.tile([P, SLOTS, D], F32, name="xn")
+            for s in slots:
                 nc.gpsimd.tensor_scalar(
-                    out=xn[:, s, :],
+                    out=live["xn", group][:, s, :],
                     in0=live["x", group][:, s, :],
                     scalar1=live["neg_mean", group][:, s : s + 1],
                     scalar2=live["rstd", group][:, s : s + 1],
                     op0=ALU.add,
                     op1=ALU.mult,
                 )
-            live["xn", group] = xn
+
+        def chunks_ahead(group):
+            return BANKS_FOR_TRANSPOSES if group == len(FIRST_SIZES) else 1
 
         def transpose_chunks(group, chunks):
             by_chunk = live["xn", group][:].rearrange("p s (u k t) -> p s u t k", u=PASSES, t=PACK)
@@ -219,18 +240,25 @@ def tile_minitransformerlayer_pa_t_kernel(tc, x, pe, w_qkv, g1, b1, out_0, out_1
                     )
                 live["xn_t", group, c] = xn_t
 
-        def scale_and_shift(group):
+        def scalar_chunks(group):
+            if group >= len(groups) - GROUPS_AT_END:
+                return CHUNKS - VECTOR_CHUNKS_AT_END
+            return CHUNKS - 1 if groups[group][2] == SLOTS and group % 4 == 0 else CHUNKS
+
+        def scale_and_shift(group, chunks, engine):
             tokens = groups[group][2] * P
-            h_chunks = h_pool.tile([P, CHUNKS, TOKENS], BF16, name="h_chunks")
-            for c in range(CHUNKS):
-                nc.scalar.activation(
-                    out=h_chunks[:, c, 0:tokens],
-                    in_=live["xn_t", group, c][:, 0:tokens],
-                    func=ACT.Identity,
-                    scale=gain_bias[:, c : c + 1],
-                    bias=gain_bias[:, CHUNKS + c : CHUNKS + c + 1],
-                )
-            live["h_chunks", group] = h_chunks
+            if ("h_chunks", group) not in live:
+                live["h_chunks", group] = h_pool.tile([P, CHUNKS, TOKENS], BF16, name="h_chunks")
+            for c in chunks:
+                out = live["h_chunks", group][:, c, 0:tokens]
+                in_ = live["xn_t", group, c][:, 0:tokens]
+                gain, bias = gain_bias[:, c : c + 1], gain_bias[:, CHUNKS + c : CHUNKS + c + 1]
+                if engine is nc.scalar:
+                    nc.scalar.activation(out=out, in_=in_, func=ACT.Identity, scale=gain, bias=bias)
+                else:
+                    nc.vector.tensor_scalar(
+                        out=out, in0=in_, scalar1=gain, scalar2=bias, op0=ALU.mult, op1=ALU.add
+                    )
 
         def regroup(group, u):
             tokens = groups[group][2] * P
@@ -238,22 +266,25 @@ def tile_minitransformerlayer_pa_t_kernel(tc, x, pe, w_qkv, g1, b1, out_0, out_1
                 live["h_grouped", group] = h_pool.tile(
                     [P, PASSES, tokens, PACK], BF16, name="h_grouped", align_bytes=64
                 )
-            nc.scalar.copy(
-                out=live["h_grouped", group][:, u, 0:tokens, :].rearrange("p (n i) t -> p n t i", i=4),
-                in_=live["h_chunks", group][:, u * PACK : (u + 1) * PACK, 0:tokens].rearrange(
-                    "p t (n i) -> p n t i", i=4
-                ),
+            out = live["h_grouped", group][:, u, 0:tokens, :].rearrange("p (n i) t -> p n t i", i=4)
+            in_ = live["h_chunks", group][:, u * PACK : (u + 1) * PACK, 0:tokens].rearrange(
+                "p t (n i) -> p n t i", i=4
             )
+            if group == len(groups) - 1 and u == PASSES - 1:
+                nc.vector.tensor_copy(out=out, in_=in_)
+            else:
+                nc.scalar.copy(out=out, in_=in_)
 
         def quantise(group):
             tokens = groups[group][2] * P
             h_codes = mx_pool.tile([P, PASSES, tokens], U32, name="h_codes", align_bytes=64)
             h_scales = mx_pool.tile([P, PASSES, tokens], U8, name="h_scales", align_bytes=64)
-            nc.vector.quantize_mx(
-                out=h_codes[:].rearrange("p u n -> p (u n)").bitcast(FP8X4),
-                scales=h_scales[:].rearrange("p u n -> p (u n)"),
-                in_=live["h_grouped", group][:].rearrange("p u n t -> p (u n t)"),
-            )
+            for u in range(PASSES):
+                nc.vector.quantize_mx(
+                    out=h_codes[:, u, :].bitcast(FP8X4),
+                    scales=h_scales[:, u, :],
+                    in_=live["h_grouped", group][:, u].rearrange("p n t -> p (n t)"),
+                )
             live["h_codes", group] = h_codes
             live["h_scales", group] = h_scales
 
@@ -325,10 +356,12 @@ def tile_minitransformerlayer_pa_t_kernel(tc, x, pe, w_qkv, g1, b1, out_0, out_1
 
         def copy_v(group):
             count = groups[group][2]
-            nc.vector.tensor_copy(
-                out=live["result", group][:, ROTATED : 3 * H, 0:count, :].rearrange("p a s d -> p s a d"),
-                in_=live["v_ps", group][:, 0:count, :].rearrange("p s (a d) -> p s a d", a=H),
-            )
+            out = live["result", group][:, ROTATED : 3 * H, 0:count, :].rearrange("p a s d -> p s a d")
+            in_ = live["v_ps", group][:, 0:count, :].rearrange("p s (a d) -> p s a d", a=H)
+            if group == len(groups) - 1:
+                nc.scalar.copy(out=out, in_=in_)
+            else:
+                nc.vector.tensor_copy(out=out, in_=in_)
 
         def store(group):
             batch, first_slot, count = groups[group]
@@ -343,15 +376,15 @@ def tile_minitransformerlayer_pa_t_kernel(tc, x, pe, w_qkv, g1, b1, out_0, out_1
             return 0 <= group < len(groups)
 
         def is_last(group):
-            return group >= len(groups) - len(LAST_SIZES)
+            return group >= len(groups) - 2
 
         with tc.manual_schedule():
             nc.vector.memset(eps[:], EPS)
             make_identity(nc, ident_f32[:])
             load_group(0)
             load_gains()
-            load_group(1)
             load_weights()
+            load_group(1)
             load_group(2)
             load_tables()
 
@@ -359,42 +392,60 @@ def tile_minitransformerlayer_pa_t_kernel(tc, x, pe, w_qkv, g1, b1, out_0, out_1
                 if in_range(r + LOADS_AHEAD):
                     load_group(r + LOADS_AHEAD)
                 if in_range(r - 4) and not is_last(r - 4):
-                    for half in halves(r - 4)[1:]:
+                    for half in halves(r - 4):
                         rotation_sum(r - 4, half, nc.gpsimd)
                     store(r - 4)
-                if in_range(r):
-                    normalise(r)
                 if in_range(r - 1):
-                    transpose_chunks(r - 1, range(CHUNKS_AHEAD, CHUNKS))
-                    scale_and_shift(r - 1)
+                    transpose_chunks(r - 1, range(chunks_ahead(r - 1), CHUNKS))
+                if r == 1:
+                    scale_and_shift(r - 1, range(2), nc.scalar)
+                    reciprocal_std(r, slots_at_once(r)[0])
+                if in_range(r):
+                    for slots in slots_at_once(r):
+                        if slots.start > 0:
+                            negated_mean(r, slots)
+                        if r > 0 or slots.start > 0:
+                            normalise(r, slots)
+                if in_range(r - 1):
+                    scale_and_shift(r - 1, range(2 if r == 1 else 0, scalar_chunks(r - 1)), nc.scalar)
+                if r == 2:
+                    quantise_weights()
                 if in_range(r - 3):
-                    for half in halves(r - 3):
+                    rotation_products(r - 3, 0)
+                if in_range(r - 2):
+                    quantise(r - 2)
+                if in_range(r - 3):
+                    for half in halves(r - 3)[1:]:
                         rotation_products(r - 3, half)
-                if in_range(r + 1):
-                    negated_mean(r + 1)
-                    reciprocal_std(r + 1)
+                if in_range(r - 1):
+                    scale_and_shift(r - 1, range(scalar_chunks(r - 1), CHUNKS), nc.vector)
+                early = slots_at_once(r + 1) if in_range(r + 1) and r != 0 else []
+                late = early[-1:] if r <= ROUNDS_TO_FILL else []
+                for slots in early[: len(early) - len(late)]:
+                    reciprocal_std(r + 1, slots)
                 if in_range(r - 1):
                     regroup(r - 1, 0)
                     regroup(r - 1, 1)
+                for slots in late:
+                    reciprocal_std(r + 1, slots)
+                if in_range(r + 1) and r >= 0:
+                    negated_mean(r + 1, slots_at_once(r + 1)[0])
                 if in_range(r):
-                    transpose_chunks(r, range(CHUNKS_AHEAD))
-                if r == 2:
-                    quantise_weights()
+                    transpose_chunks(r, range(chunks_ahead(r)))
                 if in_range(r - 2):
-                    quantise(r - 2)
                     project(r - 2)
-                if in_range(r - 3):
-                    rotation_sum(r - 3, 0, nc.vector)
                 if in_range(r - 3) and is_last(r - 3):
-                    for half in halves(r - 3)[1:]:
+                    for half in halves(r - 3):
                         rotation_sum(r - 3, half, nc.vector)
                     copy_v(r - 3)
                     store(r - 3)
+                if r == -1:
+                    normalise_on_vector(0, 0)
                 if in_range(r + 2):
                     statistics(r + 2)
                 if r == -1:
                     transpose_constants()
-                if r == 0:
+                if r == 2:
                     rotation_tables()
                 if in_range(r - 3) and not is_last(r - 3):
                     copy_v(r - 3)

from contextlib import ExitStack

import concourse.mybir as mybir
from concourse.masks import make_identity

F32 = mybir.dt.float32
BF16 = mybir.dt.bfloat16
U32 = mybir.dt.uint32
U8 = mybir.dt.uint8
FP8X4 = mybir.dt.float8_e4m3fn_x4
ALU = mybir.AluOpType
ACT = mybir.ActivationFunctionType

B, S, D, H, DH = 4, 2048, 1024, 2, 64
EPS = 1e-5
P = 128
PACK = 4
PASSES = D // (P * PACK)
CHUNKS = D // P
SLOTS_PER_BATCH = S // P
SLOTS = 4
TOKENS = SLOTS * P
GROUPS_PER_BATCH = SLOTS_PER_BATCH // SLOTS
PAIRS = DH // 2
ROTATED = 2 * H
QK_COLS = ROTATED * DH
V_COLS = H * DH
OUT_COLS = QK_COLS + V_COLS
BN_MAX = 512
BN_VALUES = 6
LOADS_AHEAD = 5
FIRST_SIZES = [2, 2]
LAST_SIZES = [2, 1, 1]
BANKS_FOR_TRANSPOSES = 4
GROUPS_AT_END = 4
VECTOR_CHUNKS_AT_END = 3
ROUNDS_TO_FILL = 2

FLOPS = 2 * B * S * D * OUT_COLS


def tile_minitransformerlayer_pa_t_kernel(tc, x, pe, w_qkv, g1, b1, out_0, out_1, out_2):
    nc = tc.nc
    outs = (out_0, out_1, out_2)

    with ExitStack() as ctx:
        const = ctx.enter_context(tc.tile_pool(name="const", bufs=1))
        x_pool = ctx.enter_context(tc.tile_pool(name="x_pool", bufs=LOADS_AHEAD + 2))
        small = ctx.enter_context(tc.tile_pool(name="small", bufs=5))
        xn_pool = ctx.enter_context(tc.tile_pool(name="xn_pool", bufs=2))
        h_pool = ctx.enter_context(tc.tile_pool(name="h_pool", bufs=2))
        mx_pool = ctx.enter_context(tc.tile_pool(name="mx_pool", bufs=2))
        rot_pool = ctx.enter_context(tc.tile_pool(name="rot_pool", bufs=4))
        res_pool = ctx.enter_context(tc.tile_pool(name="res_pool", bufs=3))

        groups = []
        for batch in range(B):
            sizes = [SLOTS] * GROUPS_PER_BATCH
            if batch == 0:
                sizes[0:1] = FIRST_SIZES
            if batch == B - 1:
                sizes[-1:] = LAST_SIZES
            first_slot = 0
            for count in sizes:
                groups.append((batch, first_slot, count))
                first_slot += count

        def halves(group):
            return range((groups[group][2] + 1) // 2)

        def slots_of_half(group, half):
            return min(2, groups[group][2] - 2 * half)

        live = {}

        def load_group(group):
            batch, first_slot, count = groups[group]
            x_sb = x_pool.tile([P, SLOTS, D], BF16, name="x_sb")
            by_slot = x[batch].rearrange("(p t) k -> p t k", t=SLOTS_PER_BATCH)
            for s in range(count):
                nc.sync.dma_start(out=x_sb[:, s, :], in_=by_slot[:, first_slot + s, :])
            live["x", group] = x_sb

        xt_psum = ctx.enter_context(tc.psum_pool(name="xt_psum", bufs=BANKS_FOR_TRANSPOSES))
        qk_psum = ctx.enter_context(tc.psum_pool(name="qk_psum", bufs=2))
        v_psum = ctx.enter_context(tc.psum_pool(name="v_psum", bufs=2))

        ident_f32 = const.tile([P, P], F32, name="ident_f32")
        eps = const.tile([P, 1], F32, name="eps")
        gain_bf16 = const.tile([P, PASSES, PACK], BF16, name="gain_bf16")
        bias_bf16 = const.tile([P, PASSES, PACK], BF16, name="bias_bf16")
        w_sb = const.tile([P, OUT_COLS // P, D], BF16, name="w_sb")
        pe_sb = const.tile([P, SLOTS_PER_BATCH, PAIRS, 2], BF16, name="pe_sb")
        c_twice = const.tile([P, SLOTS_PER_BATCH, PAIRS, 2], F32, name="c_twice")
        d_signed = const.tile([P, SLOTS_PER_BATCH, PAIRS, 2], F32, name="d_signed")
        gain_bias = const.tile([P, 2 * CHUNKS], F32, name="gain_bias")
        w_grouped = const.tile([P, PASSES, OUT_COLS, PACK], BF16, name="w_grouped", align_bytes=64)
        w_codes = const.tile([P, PASSES, OUT_COLS], U32, name="w_codes", align_bytes=64)
        w_scales = const.tile([P, PASSES, OUT_COLS], U8, name="w_scales", align_bytes=64)

        def load_gains():
            for landed, vec in ((gain_bf16, g1), (bias_bf16, b1)):
                nc.sync.dma_start(out=landed[:], in_=vec.rearrange("(u p t) -> p u t", p=P, t=PACK))

        def load_weights():
            nc.sync.dma_start(out=w_sb[:], in_=w_qkv.rearrange("(i p) k -> p i k", p=P))

        def load_tables():
            nc.sync.dma_start(
                out=pe_sb[:], in_=pe.rearrange("(p t) (j e) -> p t j e", t=SLOTS_PER_BATCH, e=2)
            )

        def rotation_tables():
            nc.gpsimd.tensor_scalar(
                out=c_twice[:],
                in0=pe_sb[:, :, :, 0:1].to_broadcast([P, SLOTS_PER_BATCH, PAIRS, 2]),
                scalar1=1.0,
                scalar2=0.0,
                op0=ALU.mult,
                op1=ALU.add,
            )
            for member, sign in ((0, -1.0), (1, 1.0)):
                nc.gpsimd.tensor_scalar(
                    out=d_signed[:, :, :, member],
                    in0=pe_sb[:, :, :, 1],
                    scalar1=sign,
                    scalar2=0.0,
                    op0=ALU.mult,
                    op1=ALU.add,
                )

        def transpose_constants():
            for first, landed in ((0, gain_bf16), (CHUNKS, bias_bf16)):
                nc.vector.tensor_copy(
                    out=gain_bias[:, first : first + CHUNKS], in_=landed[:].rearrange("p u t -> p (u t)")
                )
            w_words = w_sb[:].bitcast(F32)
            pass_words = D // 2 // PASSES
            for u in range(PASSES):
                for i in range(OUT_COLS // P):
                    w_t = xt_psum.tile([P, 2, P], F32, name="w_t", tag="xn_t")
                    for e in range(2):
                        nc.tensor.transpose(
                            w_t[:, e, :],
                            w_words[:, i, u * pass_words + e : (u + 1) * pass_words : 2],
                            ident_f32[:],
                        )
                    nc.scalar.copy(
                        out=w_grouped[:, u, i * P : (i + 1) * P, :].rearrange("p n t -> p (n t)").bitcast(F32),
                        in_=w_t[:].rearrange("p e n -> p n e"),
                    )

        def quantise_weights():
            for u in range(PASSES):
                for i in range(OUT_COLS // P):
                    rows = slice(i * P, (i + 1) * P)
                    nc.vector.quantize_mx(
                        out=w_codes[:, u, rows].bitcast(FP8X4),
                        scales=w_scales[:, u, rows],
                        in_=w_grouped[:, u, rows, :].rearrange("p n t -> p (n t)"),
                    )

        def slots_at_once(group):
            count = groups[group][2]
            step = 1 if group == 0 else 2 if group == len(FIRST_SIZES) else count
            return [range(s, s + step) for s in range(0, count, step)]

        def statistics(group):
            count = groups[group][2]
            x_sb = live["x", group]
            stats = small.tile([P, SLOTS, D // BN_MAX, BN_VALUES], F32, name="stats")
            mean_var = small.tile([P, SLOTS, 2], F32, name="mean_var")
            for slots in slots_at_once(group):
                for s in slots:
                    for part in range(D // BN_MAX):
                        nc.vector.bn_stats(
                            out=stats[:, s, part, :], in_=x_sb[:, s, part * BN_MAX : (part + 1) * BN_MAX]
                        )
                for s in slots:
                    nc.vector.bn_aggr(out=mean_var[:, s, :], in_=stats[:, s].rearrange("p a c -> p (a c)"))
            live["mean_var", group] = mean_var

        def reciprocal_std(group, slots):
            if ("rstd", group) not in live:
                live["rstd", group] = small.tile([P, SLOTS], F32, name="rstd")
            nc.scalar.activation(
                out=live["rstd", group][:, slots.start : slots.stop],
                in_=live["mean_var", group][:, slots.start : slots.stop, 1],
                func=ACT.Abs_reciprocal_sqrt,
                bias=eps[:],
                scale=1.0,
            )

        def negated_mean(group, slots):
            if ("neg_mean", group) not in live:
                live["neg_mean", group] = small.tile([P, SLOTS], F32, name="neg_mean")
            nc.gpsimd.tensor_scalar(
                out=live["neg_mean", group][:, slots.start : slots.stop],
                in0=live["mean_var", group][:, slots.start : slots.stop, 0],
                scalar1=-1.0,
                scalar2=0.0,
                op0=ALU.mult,
                op1=ALU.add,
            )

        def normalise_on_vector(group, slot):
            live["xn", group] = xn_pool.tile([P, SLOTS, D], F32, name="xn")
            nc.vector.tensor_scalar(
                out=live["xn", group][:, slot, :],
                in0=live["x", group][:, slot, :],
                scalar1=live["mean_var", group][:, slot, 0:1],
                scalar2=live["rstd", group][:, slot : slot + 1],
                op0=ALU.subtract,
                op1=ALU.mult,
            )

        def normalise(group, slots):
            if ("xn", group) not in live:
                live["xn", group] = xn_pool.tile([P, SLOTS, D], F32, name="xn")
            for s in slots:
                nc.gpsimd.tensor_scalar(
                    out=live["xn", group][:, s, :],
                    in0=live["x", group][:, s, :],
                    scalar1=live["neg_mean", group][:, s : s + 1],
                    scalar2=live["rstd", group][:, s : s + 1],
                    op0=ALU.add,
                    op1=ALU.mult,
                )

        def chunks_ahead(group):
            return BANKS_FOR_TRANSPOSES if group == len(FIRST_SIZES) else 1

        def transpose_chunks(group, chunks):
            by_chunk = live["xn", group][:].rearrange("p s (u k t) -> p s u t k", u=PASSES, t=PACK)
            for c in chunks:
                xn_t = xt_psum.tile([P, TOKENS], F32, name="xn_t")
                for s in range(groups[group][2]):
                    nc.tensor.transpose(
                        xn_t[:, s * P : (s + 1) * P], by_chunk[:, s, c // PACK, c % PACK, :], ident_f32[:]
                    )
                live["xn_t", group, c] = xn_t

        def scalar_chunks(group):
            if group >= len(groups) - GROUPS_AT_END:
                return CHUNKS - VECTOR_CHUNKS_AT_END
            return CHUNKS - 1 if groups[group][2] == SLOTS and group % 4 == 0 else CHUNKS

        def scale_and_shift(group, chunks, engine):
            tokens = groups[group][2] * P
            if ("h_chunks", group) not in live:
                live["h_chunks", group] = h_pool.tile([P, CHUNKS, TOKENS], BF16, name="h_chunks")
            for c in chunks:
                out = live["h_chunks", group][:, c, 0:tokens]
                in_ = live["xn_t", group, c][:, 0:tokens]
                gain, bias = gain_bias[:, c : c + 1], gain_bias[:, CHUNKS + c : CHUNKS + c + 1]
                if engine is nc.scalar:
                    nc.scalar.activation(out=out, in_=in_, func=ACT.Identity, scale=gain, bias=bias)
                else:
                    nc.vector.tensor_scalar(
                        out=out, in0=in_, scalar1=gain, scalar2=bias, op0=ALU.mult, op1=ALU.add
                    )

        def regroup(group, u):
            tokens = groups[group][2] * P
            if u == 0:
                live["h_grouped", group] = h_pool.tile(
                    [P, PASSES, tokens, PACK], BF16, name="h_grouped", align_bytes=64
                )
            out = live["h_grouped", group][:, u, 0:tokens, :].rearrange("p (n i) t -> p n t i", i=4)
            in_ = live["h_chunks", group][:, u * PACK : (u + 1) * PACK, 0:tokens].rearrange(
                "p t (n i) -> p n t i", i=4
            )
            if group == len(groups) - 1 and u == PASSES - 1:
                nc.vector.tensor_copy(out=out, in_=in_)
            else:
                nc.scalar.copy(out=out, in_=in_)

        def quantise(group):
            tokens = groups[group][2] * P
            h_codes = mx_pool.tile([P, PASSES, tokens], U32, name="h_codes", align_bytes=64)
            h_scales = mx_pool.tile([P, PASSES, tokens], U8, name="h_scales", align_bytes=64)
            for u in range(PASSES):
                nc.vector.quantize_mx(
                    out=h_codes[:, u, :].bitcast(FP8X4),
                    scales=h_scales[:, u, :],
                    in_=live["h_grouped", group][:, u].rearrange("p n t -> p (n t)"),
                )
            live["h_codes", group] = h_codes
            live["h_scales", group] = h_scales

        def project(group):
            h_codes, h_scales = live["h_codes", group], live["h_scales", group]
            v_ps = v_psum.tile([P, SLOTS, V_COLS], F32, name="v_ps")
            live["v_ps", group] = v_ps
            for half in halves(group):
                qk_ps = qk_psum.tile([P, 2, QK_COLS], F32, name="qk_ps")
                live["qk_ps", group, half] = qk_ps
                for i in range(slots_of_half(group, half)):
                    s = 2 * half + i
                    tokens = slice(s * P, (s + 1) * P)
                    for acc, cols in (
                        (qk_ps[:, i, :], slice(0, QK_COLS)),
                        (v_ps[:, s, :], slice(QK_COLS, OUT_COLS)),
                    ):
                        for u in range(PASSES):
                            nc.tensor.matmul_mx(
                                out=acc,
                                lhsT=h_codes[:, u, tokens].bitcast(FP8X4),
                                lhsT_scale=h_scales[:, u, tokens],
                                rhs=w_codes[:, u, cols].bitcast(FP8X4),
                                rhs_scale=w_scales[:, u, cols],
                                start=(u == 0),
                                stop=(u == PASSES - 1),
                            )

        def rotation_products(group, half):
            if half == 0:
                live["result", group] = res_pool.tile([P, 3 * H, SLOTS, DH], F32, name="result")
            count = slots_of_half(group, half)
            first_slot = groups[group][1] + 2 * half
            slots = slice(first_slot, first_slot + count)
            qk_ps = live["qk_ps", group, half][:, 0:count]
            rotated = live["result", group][:, 0:ROTATED, 2 * half : 2 * half + count, :]
            nc.vector.tensor_tensor(
                out=rotated.rearrange("p a i d -> p i a d"),
                in0=qk_ps.rearrange("p i (a d) -> p i a d", a=ROTATED),
                in1=c_twice[:, slots]
                .rearrange("p i j e -> p i (j e)")
                .unsqueeze(2)
                .to_broadcast([P, count, ROTATED, DH]),
                op=ALU.mult,
            )
            by_pair = qk_ps.rearrange("p i (a j e) -> p i a j e", a=ROTATED, e=2)
            crossed = rot_pool.tile([P, 2, ROTATED, PAIRS, 2], F32, name="crossed")
            nc.vector.tensor_tensor(
                out=crossed[:, 0:count],
                in0=by_pair[:, :, :, :, ::-1],
                in1=d_signed[:, slots]
                .rearrange("p i j e -> p i (j e)")
                .unsqueeze(2)
                .to_broadcast([P, count, ROTATED, DH])
                .rearrange("p i a (j e) -> p i a j e", e=2),
                op=ALU.mult,
            )
            live["crossed", group, half] = crossed

        def rotation_sum(group, half, engine):
            count = slots_of_half(group, half)
            rotated = live["result", group][:, 0:ROTATED, 2 * half : 2 * half + count, :]
            engine.tensor_tensor(
                out=rotated.rearrange("p a i d -> p i a d"),
                in0=rotated.rearrange("p a i d -> p i a d"),
                in1=live["crossed", group, half][:, 0:count].rearrange("p i a j e -> p i a (j e)"),
                op=ALU.add,
            )

        def copy_v(group):
            count = groups[group][2]
            out = live["result", group][:, ROTATED : 3 * H, 0:count, :].rearrange("p a s d -> p s a d")
            in_ = live["v_ps", group][:, 0:count, :].rearrange("p s (a d) -> p s a d", a=H)
            if group == len(groups) - 1:
                nc.scalar.copy(out=out, in_=in_)
            else:
                nc.vector.tensor_copy(out=out, in_=in_)

        def store(group):
            batch, first_slot, count = groups[group]
            for which in range(3):
                by_slot = outs[which][batch].rearrange("h (p t) d -> p h t d", t=SLOTS_PER_BATCH)
                nc.sync.dma_start(
                    out=by_slot[:, :, first_slot : first_slot + count, :],
                    in_=live["result", group][:, which * H : (which + 1) * H, 0:count, :],
                )

        def in_range(group):
            return 0 <= group < len(groups)

        def is_last(group):
            return group >= len(groups) - 2

        with tc.manual_schedule():
            nc.vector.memset(eps[:], EPS)
            make_identity(nc, ident_f32[:])
            load_group(0)
            load_gains()
            load_weights()
            load_group(1)
            load_group(2)
            load_tables()

            for r in range(-2, len(groups) + 3):
                if in_range(r + LOADS_AHEAD):
                    load_group(r + LOADS_AHEAD)
                if in_range(r - 4) and not is_last(r - 4):
                    for half in halves(r - 4):
                        rotation_sum(r - 4, half, nc.gpsimd)
                    store(r - 4)
                if in_range(r - 1):
                    transpose_chunks(r - 1, range(chunks_ahead(r - 1), CHUNKS))
                if r == 1:
                    scale_and_shift(r - 1, range(2), nc.scalar)
                    reciprocal_std(r, slots_at_once(r)[0])
                if in_range(r):
                    for slots in slots_at_once(r):
                        if slots.start > 0:
                            negated_mean(r, slots)
                        if r > 0 or slots.start > 0:
                            normalise(r, slots)
                if in_range(r - 1):
                    scale_and_shift(r - 1, range(2 if r == 1 else 0, scalar_chunks(r - 1)), nc.scalar)
                if r == 2:
                    quantise_weights()
                if in_range(r - 3):
                    rotation_products(r - 3, 0)
                if in_range(r - 2):
                    quantise(r - 2)
                if in_range(r - 3):
                    for half in halves(r - 3)[1:]:
                        rotation_products(r - 3, half)
                if in_range(r - 1):
                    scale_and_shift(r - 1, range(scalar_chunks(r - 1), CHUNKS), nc.vector)
                early = slots_at_once(r + 1) if in_range(r + 1) and r != 0 else []
                late = early[-1:] if r <= ROUNDS_TO_FILL else []
                for slots in early[: len(early) - len(late)]:
                    reciprocal_std(r + 1, slots)
                if in_range(r - 1):
                    regroup(r - 1, 0)
                    regroup(r - 1, 1)
                for slots in late:
                    reciprocal_std(r + 1, slots)
                if in_range(r + 1) and r >= 0:
                    negated_mean(r + 1, slots_at_once(r + 1)[0])
                if in_range(r):
                    transpose_chunks(r, range(chunks_ahead(r)))
                if in_range(r - 2):
                    project(r - 2)
                if in_range(r - 3) and is_last(r - 3):
                    for half in halves(r - 3):
                        rotation_sum(r - 3, half, nc.vector)
                    copy_v(r - 3)
                    store(r - 3)
                if r == -1:
                    normalise_on_vector(0, 0)
                if in_range(r + 2):
                    statistics(r + 2)
                if r == -1:
                    transpose_constants()
                if r == 2:
                    rotation_tables()
                if in_range(r - 3) and not is_last(r - 3):
                    copy_v(r - 3)
